import numpy as np
import ml_dtypes


def mxq(x, axis, fmt="e4m3"):
    dtype, down = {"e4m3": (ml_dtypes.float8_e4m3fn, 7), "e5m2": (ml_dtypes.float8_e5m2, 14)}[fmt]
    v = np.moveaxis(np.asarray(x, np.float32).astype(ml_dtypes.bfloat16).astype(np.float64), axis, -1)
    blocks = v.reshape(v.shape[:-1] + (-1, 32))
    amax = np.abs(blocks).max(-1, keepdims=True)
    byte = np.maximum(np.where(amax > 0, np.frexp(amax)[1] - 1 + 127, 0) - down, 1)
    scale = np.exp2(byte - 127.0)
    codes = (blocks / scale).astype(np.float32).astype(dtype).astype(np.float64)
    return np.moveaxis((codes * scale).reshape(v.shape), -1, axis)


WIDE = False


def mx_kscale(k):
    if not WIDE:
        return np.ones(k)
    levels = np.array([10, -10, 5, -5, 0])
    a = np.random.permutation(np.resize(levels, k // 512 * 4)).reshape(k // 512, 4)
    idx = np.arange(k)
    return np.exp2(a[idx // 512, idx % 128 // 32])


BF16 = ml_dtypes.bfloat16


def bf(x):
    return np.asarray(x, np.float32).astype(BF16)


def f64(x):
    return np.asarray(x).astype(np.float64)


E2M1 = np.array([0.0, 0.5, 1.0, 1.5, 2.0, 3.0, 4.0, 6.0, -0.0, -0.5, -1.0, -1.5, -2.0, -3.0, -4.0, -6.0])


def pack_weight(w, fmt):
    k, n = w.shape
    w = f64(bf(w)).reshape(k // 32, 32, n)
    amax = np.abs(w).max(1)
    if fmt == "e4m3":
        byte = np.frexp(amax)[1] - 1 + 127 - 7
    else:
        mant, ex = np.frexp(amax / 6.0)
        byte = np.where(mant > 0.5, ex, ex - 1) + 127
    byte = np.clip(np.where(amax > 0, byte, 1), 1, 254)
    scaled = (w * np.exp2(127.0 - byte)[:, None, :]).reshape(k, n).astype(np.float32)
    by_word = np.ascontiguousarray(scaled.reshape(k // 512, 128, 4, n).transpose(0, 1, 3, 2))
    if fmt == "e4m3":
        words = by_word.astype(ml_dtypes.float8_e4m3fn).view(np.uint8)
    else:
        c = by_word.astype(ml_dtypes.float4_e2m1fn).view(np.uint8) & 0xF
        words = c[..., 0::2] | (c[..., 1::2] << 4)
    return np.ascontiguousarray(words), np.ascontiguousarray(byte.astype(np.uint8).reshape(k // 512, 16, n))


def unpack_weight(words, scales, fmt):
    g, p, n, _ = words.shape
    if fmt == "e4m3":
        vals = np.ascontiguousarray(words).view(ml_dtypes.float8_e4m3fn).astype(np.float64)
    else:
        nib = np.empty((g, p, n, 4), np.uint8)
        nib[..., 0::2] = words & 0xF
        nib[..., 1::2] = words >> 4
        vals = E2M1[nib]
    vals = vals * np.repeat(np.exp2(scales.astype(np.float64) - 127.0), 8, axis=1)[..., None]
    return vals.transpose(0, 1, 3, 2).reshape(g * 512, n)


B, T, HID, H, D, QB = 1, 128, 8192, 12, 128, 512
LN_EPS = 1e-5
FMT = "e4m3"


def layer_norm(u):
    mu = u.mean(-1, keepdims=True)
    var = ((u - mu) ** 2).mean(-1, keepdims=True)
    return (u - mu) * (1.0 / np.sqrt(var + LN_EPS))


def feature_map(u, gamma, beta):
    return layer_norm(u * gamma + beta)


def setup_inputs():
    s = mx_kscale(HID)
    hidden_states = bf(np.random.standard_normal((B, T, HID)) * s)
    wq = np.random.standard_normal((H * D, HID)) / np.sqrt(HID) / s
    wk = np.random.standard_normal((H * D, HID)) / np.sqrt(HID) / s
    gamma = bf(1.0 + 0.1 * np.random.standard_normal(D))
    beta = bf(0.1 * np.random.standard_normal(D))
    wq_words, wq_scales = pack_weight(np.ascontiguousarray(wq.T), FMT)
    wk_words, wk_scales = pack_weight(np.ascontiguousarray(wk.T), FMT)
    return {"hidden_states": hidden_states,
            "Wq_words": wq_words,
            "Wq_scales": wq_scales,
            "Wk_words": wk_words,
            "Wk_scales": wk_scales,
            "gamma": gamma,
            "beta": beta}


def reference(hidden_states, Wq_words, Wq_scales, Wk_words, Wk_scales, gamma, beta):
    g, b = f64(gamma), f64(beta)
    xq = mxq(f64(hidden_states), 2, "e4m3")
    q = (xq @ unpack_weight(Wq_words, Wq_scales, FMT)).reshape(B, T, H, D)
    k = (xq @ unpack_weight(Wk_words, Wk_scales, FMT)).reshape(B, T, H, D)
    q_feat = feature_map(q, g, b) * (D ** -0.5)
    k_feat = feature_map(k, g, b)
    return q_feat, k_feat

@@ -1,0 +1,199 @@
+from contextlib import ExitStack
+
+import concourse.mybir as mybir
+from concourse.masks import make_identity
+
+F32 = mybir.dt.float32
+BF16 = mybir.dt.bfloat16
+I32 = mybir.dt.int32
+U32 = mybir.dt.uint32
+U8 = mybir.dt.uint8
+FP8X4 = mybir.dt.float8_e4m3fn_x4
+ALU = mybir.AluOpType
+
+P = 128
+HID = 8192
+K_PASS = 4 * P
+GROUPS = HID // K_PASS
+D = 128
+N_OUT = 12 * D
+N_TILE = 512
+CHUNKS = N_OUT // N_TILE
+HEADS_PER_CHUNK = N_TILE // D
+LN_EPS = 1e-5
+
+PLANES_PER_SLOT = 4
+SLOTS = GROUPS // PLANES_PER_SLOT
+X_PIECES = 4
+GROUPS_PER_PIECE = GROUPS // X_PIECES
+GROUPS_PER_BANK = 2
+TAIL_GROUPS = 4
+
+FLOPS = 2 * P * HID * 2 * N_OUT
+
+
+def tile_rebasedlinearattention_pa_k_kernel(
+    tc, hidden_states, Wq_words, Wq_scales, Wk_words, Wk_scales, gamma, beta, out_0, out_1
+):
+    nc = tc.nc
+    with ExitStack() as ctx:
+        const = ctx.enter_context(tc.tile_pool(name="const", bufs=1))
+        xin = ctx.enter_context(tc.tile_pool(name="xin", bufs=X_PIECES))
+        stage = ctx.enter_context(tc.tile_pool(name="stage", bufs=3))
+        wide = ctx.enter_context(tc.tile_pool(name="wide", bufs=12))
+        narrow = ctx.enter_context(tc.tile_pool(name="narrow", bufs=1))
+        work = ctx.enter_context(tc.tile_pool(name="work", bufs=3))
+        small = ctx.enter_context(tc.tile_pool(name="small", bufs=3))
+        psum_x = ctx.enter_context(tc.psum_pool(name="psum_x", bufs=2))
+        psum_acc = ctx.enter_context(tc.psum_pool(name="psum_acc", bufs=1))
+        ctx.enter_context(tc.manual_schedule())
+
+        warm = const.tile([P, 1], F32)
+        nc.vector.memset(warm[:], 1.0)
+        nc.scalar.sqrt(warm[:], warm[:])
+
+        ident = const.tile([P, P], F32)
+        make_identity(nc, ident[:])
+
+        x_rows = hidden_states[0]
+        piece_cols = HID // X_PIECES
+        x_pieces = []
+        for i in range(X_PIECES):
+            x_piece = xin.tile([P, piece_cols], BF16)
+            nc.sync.dma_start(out=x_piece[:], in_=x_rows[:, i * piece_cols : (i + 1) * piece_cols])
+            x_pieces.append(x_piece)
+
+        def load_scale_planes(planes, scales):
+            nc.vector.memset(planes[:].bitcast(I32), 0)
+            for j in range(SLOTS):
+                for quadrant in range(4):
+                    nc.sync.dma_start(
+                        out=planes[32 * quadrant : 32 * quadrant + 16, j, :].bitcast(I32),
+                        in_=scales[
+                            PLANES_PER_SLOT * j : PLANES_PER_SLOT * (j + 1),
+                            4 * quadrant : 4 * quadrant + 4,
+                            :,
+                        ].bitcast(I32),
+                    )
+
+        planes_q = const.tile([P, SLOTS, N_OUT], U8, align_bytes=64)
+        planes_k = const.tile([P, SLOTS, N_OUT], U8, align_bytes=64)
+        load_scale_planes(planes_q, Wq_scales)
+
+        gb_rows = const.tile([P, 2 * D], BF16)
+        nc.vector.memset(gb_rows[:], 0.0)
+        nc.scalar.dma_start(out=gb_rows[0:1, 0:D], in_=gamma.unsqueeze(0))
+        nc.scalar.dma_start(out=gb_rows[0:1, D : 2 * D], in_=beta.unsqueeze(0))
+        ones = const.tile([P, P], BF16)
+        nc.vector.memset(ones[:], 1.0)
+
+        x_codes = const.tile([P, GROUPS * P], U32, align_bytes=64)
+        x_planes = const.tile([P, GROUPS * P], U8, align_bytes=64)
+        for b in range(GROUPS // GROUPS_PER_BANK):
+            xt = psum_x.tile([P, GROUPS_PER_BANK, 2, P], F32, tag="bank")
+            for i in range(GROUPS_PER_BANK):
+                g = GROUPS_PER_BANK * b + i
+                pairs = x_pieces[g // GROUPS_PER_PIECE][:].bitcast(F32)
+                first = (g % GROUPS_PER_PIECE) * (K_PASS // 2)
+                for u in range(2):
+                    nc.tensor.transpose(
+                        xt[:, i, u, :], pairs[:, first + u : first + K_PASS // 2 : 2], ident[:]
+                    )
+            grouped = stage.tile([P, GROUPS_PER_BANK * K_PASS], BF16, align_bytes=64)
+            nc.scalar.copy(
+                out=grouped[:].bitcast(F32).rearrange("p (g t u) -> p g t u", g=GROUPS_PER_BANK, u=2),
+                in_=xt[:].rearrange("p g u t -> p g t u"),
+            )
+            cols = slice(GROUPS_PER_BANK * b * P, GROUPS_PER_BANK * (b + 1) * P)
+            nc.vector.quantize_mx(
+                out=x_codes[:, cols].bitcast(FP8X4), scales=x_planes[:, cols], in_=grouped[:]
+            )
+
+        gb_bank = psum_x.tile([P, 2 * D], F32, tag="bank")
+        nc.tensor.matmul(out=gb_bank[:], lhsT=ones[:], rhs=gb_rows[:], start=True, stop=True)
+        gb = const.tile([P, 2, D], F32)
+        nc.vector.tensor_copy(out=gb[:].rearrange("p a d -> p (a d)"), in_=gb_bank[:])
+        gamma_all = gb[:, 0, :].unsqueeze(1).to_broadcast([P, HEADS_PER_CHUNK, D])
+        beta_all = gb[:, 1, :].unsqueeze(1).to_broadcast([P, HEADS_PER_CHUNK, D])
+
+        def multiply(acc, g, w_words, planes, c):
+            nc.tensor.matmul_mx(
+                out=acc[:],
+                lhsT=x_codes[:, g * P : (g + 1) * P].bitcast(FP8X4),
+                lhsT_scale=x_planes[:, g * P : (g + 1) * P],
+                rhs=w_words.bitcast(FP8X4),
+                rhs_scale=planes[
+                    4 * (g % PLANES_PER_SLOT) : P, g // PLANES_PER_SLOT, c * N_TILE : (c + 1) * N_TILE
+                ],
+                start=(g == 0),
+                stop=(g == GROUPS - 1),
+            )
+
+        def feature_map(acc, factor, out_cols, store_queue):
+            u = work.tile([P, HEADS_PER_CHUNK, D], F32)
+            nc.vector.tensor_tensor(
+                out=u[:], in0=acc[:].rearrange("p (h d) -> p h d", d=D), in1=gamma_all, op=ALU.mult
+            )
+            nc.vector.tensor_tensor(out=u[:], in0=u[:], in1=beta_all, op=ALU.add)
+            stats = small.tile([P, HEADS_PER_CHUNK, 6], F32)
+            for h in range(HEADS_PER_CHUNK):
+                nc.vector.bn_stats(out=stats[:, h, :], in_=u[:, h, :])
+            mean_var = small.tile([P, HEADS_PER_CHUNK, 2], F32)
+            for h in range(HEADS_PER_CHUNK):
+                nc.vector.bn_aggr(out=mean_var[:, h, :], in_=stats[:, h, :])
+            spread = small.tile([P, HEADS_PER_CHUNK], F32)
+            nc.vector.tensor_scalar(
+                out=spread[:],
+                in0=mean_var[:, :, 1],
+                scalar1=1.0 / factor**2,
+                scalar2=LN_EPS / factor**2,
+                op0=ALU.mult,
+                op1=ALU.add,
+            )
+            nc.scalar.sqrt(spread[:], spread[:])
+            gain = small.tile([P, HEADS_PER_CHUNK], F32)
+            nc.vector.reciprocal(gain[:], spread[:])
+            f = work.tile([P, HEADS_PER_CHUNK, D], F32)
+            for h in range(HEADS_PER_CHUNK):
+                nc.vector.tensor_scalar(
+                    out=f[:, h, :],
+                    in0=u[:, h, :],
+                    scalar1=mean_var[:, h, 0:1],
+                    scalar2=gain[:, h : h + 1],
+                    op0=ALU.subtract,
+                    op1=ALU.mult,
+                )
+            store_queue.dma_start(out=out_cols, in_=f[:].rearrange("p h d -> p (h d)"))
+
+        q_words = Wq_words.rearrange("g p n t -> g p (n t)").bitcast(I32)
+        k_words = Wk_words.rearrange("g p n t -> g p (n t)").bitcast(I32)
+        q_out = out_0[0].rearrange("t h d -> t (h d)")
+        k_out = out_1[0].rearrange("t h d -> t (h d)")
+
+        def whole_group(acc, g, words, planes):
+            w = wide.tile([P, N_OUT], U32, align_bytes=64)
+            nc.sync.dma_start(out=w[:].bitcast(I32), in_=words[g])
+            for c in range(CHUNKS):
+                multiply(acc[c], g, w[:, c * N_TILE : (c + 1) * N_TILE], planes, c)
+
+        acc_q = [psum_acc.tile([P, N_TILE], F32, name="acc_q%d" % c) for c in range(CHUNKS)]
+        for g in range(GROUPS):
+            whole_group(acc_q, g, q_words, planes_q)
+        load_scale_planes(planes_k, Wk_scales)
+        for c in range(CHUNKS):
+            feature_map(acc_q[c], D**-0.5, q_out[:, c * N_TILE : (c + 1) * N_TILE], nc.scalar)
+
+        acc_k = [psum_acc.tile([P, N_TILE], F32, name="acc_k%d" % c) for c in range(CHUNKS)]
+        for g in range(GROUPS - TAIL_GROUPS):
+            whole_group(acc_k, g, k_words, planes_k)
+        tail = {}
+        for c in range(CHUNKS):
+            for g in range(GROUPS - TAIL_GROUPS, GROUPS):
+                tail[(c, g)] = narrow.tile([P, N_TILE], U32, name="tail_%d_%d" % (c, g), align_bytes=64)
+                nc.sync.dma_start(
+                    out=tail[(c, g)][:].bitcast(I32), in_=k_words[g, :, c * N_TILE : (c + 1) * N_TILE]
+                )
+        for c in range(CHUNKS):
+            for g in range(GROUPS - TAIL_GROUPS, GROUPS):
+                multiply(acc_k[c], g, tail[(c, g)][:], planes_k, c)
+            feature_map(acc_k[c], 1.0, k_out[:, c * N_TILE : (c + 1) * N_TILE], nc.sync)

@@ -67,18 +67,19 @@ def tile_rebasedlinearattention_pa_k_kernel(
             nc.vector.memset(planes[:].bitcast(I32), 0)
             for j in range(SLOTS):
                 for quadrant in range(4):
-                    nc.sync.dma_start(
-                        out=planes[32 * quadrant : 32 * quadrant + 16, j, :].bitcast(I32),
+                    nc.gpsimd.dma_start(
+                        out=planes[32 * quadrant : 32 * quadrant + 16, j, :].bitcast(F32),
                         in_=scales[
                             PLANES_PER_SLOT * j : PLANES_PER_SLOT * (j + 1),
                             4 * quadrant : 4 * quadrant + 4,
                             :,
-                        ].bitcast(I32),
+                        ].bitcast(F32),
                     )
 
         planes_q = const.tile([P, SLOTS, N_OUT], U8, align_bytes=64)
         planes_k = const.tile([P, SLOTS, N_OUT], U8, align_bytes=64)
         load_scale_planes(planes_q, Wq_scales)
+        load_scale_planes(planes_k, Wk_scales)
 
         gb_rows = const.tile([P, 2 * D], BF16)
         nc.vector.memset(gb_rows[:], 0.0)
@@ -179,7 +180,6 @@ def tile_rebasedlinearattention_pa_k_kernel(
         acc_q = [psum_acc.tile([P, N_TILE], F32, name="acc_q%d" % c) for c in range(CHUNKS)]
         for g in range(GROUPS):
             whole_group(acc_q, g, q_words, planes_q)
-        load_scale_planes(planes_k, Wk_scales)
         for c in range(CHUNKS):
             feature_map(acc_q[c], D**-0.5, q_out[:, c * N_TILE : (c + 1) * N_TILE], nc.scalar)
 

@@ -27,7 +27,7 @@ SLOTS = GROUPS // PLANES_PER_SLOT
 X_PIECES = 4
 GROUPS_PER_PIECE = GROUPS // X_PIECES
 GROUPS_PER_BANK = 2
-TAIL_GROUPS = 4
+TAIL_GROUPS = 8
 
 FLOPS = 2 * P * HID * 2 * N_OUT
 

@@ -43,6 +43,7 @@ def tile_rebasedlinearattention_pa_k_kernel(
         wide = ctx.enter_context(tc.tile_pool(name="wide", bufs=12))
         narrow = ctx.enter_context(tc.tile_pool(name="narrow", bufs=1))
         work = ctx.enter_context(tc.tile_pool(name="work", bufs=3))
+        results = ctx.enter_context(tc.tile_pool(name="results", bufs=2 * CHUNKS))
         small = ctx.enter_context(tc.tile_pool(name="small", bufs=3))
         psum_x = ctx.enter_context(tc.psum_pool(name="psum_x", bufs=2))
         psum_acc = ctx.enter_context(tc.psum_pool(name="psum_acc", bufs=1))
@@ -130,7 +131,7 @@ def tile_rebasedlinearattention_pa_k_kernel(
                 stop=(g == GROUPS - 1),
             )
 
-        def feature_map(acc, factor, out_cols, store_queue):
+        def feature_map(acc, factor):
             u = work.tile([P, HEADS_PER_CHUNK, D], F32)
             nc.vector.tensor_tensor(
                 out=u[:], in0=acc[:].rearrange("p (h d) -> p h d", d=D), in1=gamma_all, op=ALU.mult
@@ -154,7 +155,7 @@ def tile_rebasedlinearattention_pa_k_kernel(
             nc.scalar.sqrt(spread[:], spread[:])
             gain = small.tile([P, HEADS_PER_CHUNK], F32)
             nc.vector.reciprocal(gain[:], spread[:])
-            f = work.tile([P, HEADS_PER_CHUNK, D], F32)
+            f = results.tile([P, HEADS_PER_CHUNK, D], F32)
             for h in range(HEADS_PER_CHUNK):
                 nc.vector.tensor_scalar(
                     out=f[:, h, :],
@@ -164,7 +165,12 @@ def tile_rebasedlinearattention_pa_k_kernel(
                     op0=ALU.subtract,
                     op1=ALU.mult,
                 )
-            store_queue.dma_start(out=out_cols, in_=f[:].rearrange("p h d -> p (h d)"))
+            return f
+
+        def store(out_rows, c, f):
+            nc.sync.dma_start(
+                out=out_rows[:, c * N_TILE : (c + 1) * N_TILE], in_=f[:].rearrange("p h d -> p (h d)")
+            )
 
         q_words = Wq_words.rearrange("g p n t -> g p (n t)").bitcast(I32)
         k_words = Wk_words.rearrange("g p n t -> g p (n t)").bitcast(I32)
@@ -180,8 +186,7 @@ def tile_rebasedlinearattention_pa_k_kernel(
         acc_q = [psum_acc.tile([P, N_TILE], F32, name="acc_q%d" % c) for c in range(CHUNKS)]
         for g in range(GROUPS):
             whole_group(acc_q, g, q_words, planes_q)
-        for c in range(CHUNKS):
-            feature_map(acc_q[c], D**-0.5, q_out[:, c * N_TILE : (c + 1) * N_TILE], nc.scalar)
+        q_feat = [feature_map(acc_q[c], D**-0.5) for c in range(CHUNKS)]
 
         acc_k = [psum_acc.tile([P, N_TILE], F32, name="acc_k%d" % c) for c in range(CHUNKS)]
         for g in range(GROUPS - TAIL_GROUPS):
@@ -194,6 +199,8 @@ def tile_rebasedlinearattention_pa_k_kernel(
                     out=tail[(c, g)][:].bitcast(I32), in_=k_words[g, :, c * N_TILE : (c + 1) * N_TILE]
                 )
         for c in range(CHUNKS):
+            store(q_out, c, q_feat[c])
+        for c in range(CHUNKS):
             for g in range(GROUPS - TAIL_GROUPS, GROUPS):
                 multiply(acc_k[c], g, tail[(c, g)][:], planes_k, c)
-            feature_map(acc_k[c], 1.0, k_out[:, c * N_TILE : (c + 1) * N_TILE], nc.sync)
+            store(k_out, c, feature_map(acc_k[c], 1.0))

@@ -10,6 +10,7 @@ U32 = mybir.dt.uint32
 U8 = mybir.dt.uint8
 FP8X4 = mybir.dt.float8_e4m3fn_x4
 ALU = mybir.AluOpType
+ACT = mybir.ActivationFunctionType
 
 P = 128
 HID = 8192
@@ -19,7 +20,7 @@ D = 128
 N_OUT = 12 * D
 N_TILE = 512
 CHUNKS = N_OUT // N_TILE
-HEADS_PER_CHUNK = N_TILE // D
+PAIRS = N_TILE // (2 * D)
 LN_EPS = 1e-5
 
 PLANES_PER_SLOT = 4
@@ -49,9 +50,12 @@ def tile_rebasedlinearattention_pa_k_kernel(
         psum_acc = ctx.enter_context(tc.psum_pool(name="psum_acc", bufs=1))
         ctx.enter_context(tc.manual_schedule())
 
+        shift_q = const.tile([P, 1], F32)
+        nc.vector.memset(shift_q[:], LN_EPS * D)
+        shift_k = const.tile([P, 1], F32)
+        nc.vector.memset(shift_k[:], LN_EPS)
         warm = const.tile([P, 1], F32)
-        nc.vector.memset(warm[:], 1.0)
-        nc.scalar.sqrt(warm[:], warm[:])
+        nc.scalar.activation(out=warm[:], in_=shift_k[:], func=ACT.Abs_reciprocal_sqrt)
 
         ident = const.tile([P, P], F32)
         make_identity(nc, ident[:])
@@ -115,8 +119,8 @@ def tile_rebasedlinearattention_pa_k_kernel(
         nc.tensor.matmul(out=gb_bank[:], lhsT=ones[:], rhs=gb_rows[:], start=True, stop=True)
         gb = const.tile([P, 2, D], F32)
         nc.vector.tensor_copy(out=gb[:].rearrange("p a d -> p (a d)"), in_=gb_bank[:])
-        gamma_all = gb[:, 0, :].unsqueeze(1).to_broadcast([P, HEADS_PER_CHUNK, D])
-        beta_all = gb[:, 1, :].unsqueeze(1).to_broadcast([P, HEADS_PER_CHUNK, D])
+        gamma_pair = gb[:, 0, :].unsqueeze(1).to_broadcast([P, 2, D])
+        beta_pair = gb[:, 1, :].unsqueeze(1).to_broadcast([P, 2, D])
 
         def multiply(acc, g, w_words, planes, c):
             nc.tensor.matmul_mx(
@@ -131,45 +135,44 @@ def tile_rebasedlinearattention_pa_k_kernel(
                 stop=(g == GROUPS - 1),
             )
 
-        def feature_map(acc, factor):
-            u = work.tile([P, HEADS_PER_CHUNK, D], F32)
-            nc.vector.tensor_tensor(
-                out=u[:], in0=acc[:].rearrange("p (h d) -> p h d", d=D), in1=gamma_all, op=ALU.mult
-            )
-            nc.vector.tensor_tensor(out=u[:], in0=u[:], in1=beta_all, op=ALU.add)
-            stats = small.tile([P, HEADS_PER_CHUNK, 6], F32)
-            for h in range(HEADS_PER_CHUNK):
-                nc.vector.bn_stats(out=stats[:, h, :], in_=u[:, h, :])
-            mean_var = small.tile([P, HEADS_PER_CHUNK, 2], F32)
-            for h in range(HEADS_PER_CHUNK):
-                nc.vector.bn_aggr(out=mean_var[:, h, :], in_=stats[:, h, :])
-            spread = small.tile([P, HEADS_PER_CHUNK], F32)
-            nc.vector.tensor_scalar(
-                out=spread[:],
-                in0=mean_var[:, :, 1],
-                scalar1=1.0 / factor**2,
-                scalar2=LN_EPS / factor**2,
-                op0=ALU.mult,
-                op1=ALU.add,
-            )
-            nc.scalar.sqrt(spread[:], spread[:])
-            gain = small.tile([P, HEADS_PER_CHUNK], F32)
-            nc.vector.reciprocal(gain[:], spread[:])
-            f = results.tile([P, HEADS_PER_CHUNK, D], F32)
-            for h in range(HEADS_PER_CHUNK):
-                nc.vector.tensor_scalar(
-                    out=f[:, h, :],
-                    in0=u[:, h, :],
-                    scalar1=mean_var[:, h, 0:1],
-                    scalar2=gain[:, h : h + 1],
-                    op0=ALU.subtract,
-                    op1=ALU.mult,
+        def feature_map(acc, factor, shift):
+            v = acc[:].rearrange("p (a h d) -> p a h d", a=PAIRS, d=D)
+            u = work.tile([P, PAIRS, 2, D], F32)
+            for a in range(PAIRS):
+                nc.vector.tensor_tensor(out=u[:, a], in0=v[:, a], in1=gamma_pair, op=ALU.mult)
+            for a in range(PAIRS):
+                nc.vector.tensor_tensor(out=u[:, a], in0=u[:, a], in1=beta_pair, op=ALU.add)
+            stats = small.tile([P, PAIRS, 2, 6], F32)
+            mean_var = small.tile([P, PAIRS, 2, 2], F32)
+            gain = small.tile([P, PAIRS, 2], F32)
+            for a in range(PAIRS):
+                for h in range(2):
+                    nc.vector.bn_stats(out=stats[:, a, h, :], in_=u[:, a, h, :])
+                for h in range(2):
+                    nc.vector.bn_aggr(out=mean_var[:, a, h, :], in_=stats[:, a, h, :])
+                nc.scalar.activation(
+                    out=gain[:, a, :],
+                    in_=mean_var[:, a, :, 1],
+                    func=ACT.Abs_reciprocal_sqrt,
+                    bias=shift[:, 0:1],
+                    scale=1.0 / factor**2,
                 )
+            f = results.tile([P, PAIRS, 2, D], F32)
+            for a in range(PAIRS):
+                for h in range(2):
+                    nc.vector.tensor_scalar(
+                        out=f[:, a, h, :],
+                        in0=u[:, a, h, :],
+                        scalar1=mean_var[:, a, h, 0:1],
+                        scalar2=gain[:, a, h : h + 1],
+                        op0=ALU.subtract,
+                        op1=ALU.mult,
+                    )
             return f
 
         def store(out_rows, c, f):
             nc.sync.dma_start(
-                out=out_rows[:, c * N_TILE : (c + 1) * N_TILE], in_=f[:].rearrange("p h d -> p (h d)")
+                out=out_rows[:, c * N_TILE : (c + 1) * N_TILE], in_=f[:].rearrange("p a h d -> p (a h d)")
             )
 
         q_words = Wq_words.rearrange("g p n t -> g p (n t)").bitcast(I32)
@@ -186,7 +189,7 @@ def tile_rebasedlinearattention_pa_k_kernel(
         acc_q = [psum_acc.tile([P, N_TILE], F32, name="acc_q%d" % c) for c in range(CHUNKS)]
         for g in range(GROUPS):
             whole_group(acc_q, g, q_words, planes_q)
-        q_feat = [feature_map(acc_q[c], D**-0.5) for c in range(CHUNKS)]
+        q_feat = [feature_map(acc_q[c], D**-0.5, shift_q) for c in range(CHUNKS)]
 
         acc_k = [psum_acc.tile([P, N_TILE], F32, name="acc_k%d" % c) for c in range(CHUNKS)]
         for g in range(GROUPS - TAIL_GROUPS):
@@ -203,4 +206,4 @@ def tile_rebasedlinearattention_pa_k_kernel(
         for c in range(CHUNKS):
             for g in range(GROUPS - TAIL_GROUPS, GROUPS):
                 multiply(acc_k[c], g, tail[(c, g)][:], planes_k, c)
-            store(k_out, c, feature_map(acc_k[c], 1.0))
+            store(k_out, c, feature_map(acc_k[c], 1.0, shift_k))

@@ -20,7 +20,6 @@ D = 128
 N_OUT = 12 * D
 N_TILE = 512
 CHUNKS = N_OUT // N_TILE
-PAIRS = N_TILE // (2 * D)
 LN_EPS = 1e-5
 
 PLANES_PER_SLOT = 4
@@ -29,6 +28,8 @@ X_PIECES = 4
 GROUPS_PER_PIECE = GROUPS // X_PIECES
 GROUPS_PER_BANK = 2
 TAIL_GROUPS = 8
+K_UNITS = [(0, 512), (512, 512), (1024, 256), (1280, 256)]
+TAIL_LOADS = [[1] * 8, [1] * 8, [2, 2, 2, 2], [2, 2, 2, 1, 1]]
 
 FLOPS = 2 * P * HID * 2 * N_OUT
 
@@ -119,36 +120,38 @@ def tile_rebasedlinearattention_pa_k_kernel(
         nc.tensor.matmul(out=gb_bank[:], lhsT=ones[:], rhs=gb_rows[:], start=True, stop=True)
         gb = const.tile([P, 2, D], F32)
         nc.vector.tensor_copy(out=gb[:].rearrange("p a d -> p (a d)"), in_=gb_bank[:])
-        gamma_pair = gb[:, 0, :].unsqueeze(1).to_broadcast([P, 2, D])
-        beta_pair = gb[:, 1, :].unsqueeze(1).to_broadcast([P, 2, D])
 
-        def multiply(acc, g, w_words, planes, c):
+        def gb_rep(which, heads):
+            return gb[:, which, :].unsqueeze(1).to_broadcast([P, heads, D])
+
+        def multiply(acc, g, w_words, planes, first, width):
             nc.tensor.matmul_mx(
                 out=acc[:],
                 lhsT=x_codes[:, g * P : (g + 1) * P].bitcast(FP8X4),
                 lhsT_scale=x_planes[:, g * P : (g + 1) * P],
                 rhs=w_words.bitcast(FP8X4),
                 rhs_scale=planes[
-                    4 * (g % PLANES_PER_SLOT) : P, g // PLANES_PER_SLOT, c * N_TILE : (c + 1) * N_TILE
+                    4 * (g % PLANES_PER_SLOT) : P, g // PLANES_PER_SLOT, first : first + width
                 ],
                 start=(g == 0),
                 stop=(g == GROUPS - 1),
             )
 
-        def feature_map(acc, factor, shift):
-            v = acc[:].rearrange("p (a h d) -> p a h d", a=PAIRS, d=D)
-            u = work.tile([P, PAIRS, 2, D], F32)
-            for a in range(PAIRS):
-                nc.vector.tensor_tensor(out=u[:, a], in0=v[:, a], in1=gamma_pair, op=ALU.mult)
-            for a in range(PAIRS):
-                nc.vector.tensor_tensor(out=u[:, a], in0=u[:, a], in1=beta_pair, op=ALU.add)
-            stats = small.tile([P, PAIRS, 2, 6], F32)
-            mean_var = small.tile([P, PAIRS, 2, 2], F32)
-            gain = small.tile([P, PAIRS, 2], F32)
-            for a in range(PAIRS):
-                for h in range(2):
+        def feature_map(acc, heads, factor, shift):
+            each = heads // 2
+            v = acc[:].rearrange("p (a h d) -> p a h d", a=2, d=D)
+            u = work.tile([P, 2, each, D], F32, tag="u%d" % each)
+            for a in range(2):
+                nc.vector.tensor_tensor(out=u[:, a], in0=v[:, a], in1=gb_rep(0, each), op=ALU.mult)
+            for a in range(2):
+                nc.vector.tensor_tensor(out=u[:, a], in0=u[:, a], in1=gb_rep(1, each), op=ALU.add)
+            stats = small.tile([P, 2, each, 6], F32, tag="stats%d" % each)
+            mean_var = small.tile([P, 2, each, 2], F32, tag="mean_var%d" % each)
+            gain = small.tile([P, 2, each], F32, tag="gain%d" % each)
+            for a in range(2):
+                for h in range(each):
                     nc.vector.bn_stats(out=stats[:, a, h, :], in_=u[:, a, h, :])
-                for h in range(2):
+                for h in range(each):
                     nc.vector.bn_aggr(out=mean_var[:, a, h, :], in_=stats[:, a, h, :])
                 nc.scalar.activation(
                     out=gain[:, a, :],
@@ -157,9 +160,9 @@ def tile_rebasedlinearattention_pa_k_kernel(
                     bias=shift[:, 0:1],
                     scale=1.0 / factor**2,
                 )
-            f = results.tile([P, PAIRS, 2, D], F32)
-            for a in range(PAIRS):
-                for h in range(2):
+            f = results.tile([P, 2, each, D], F32, tag="f%d" % each)
+            for a in range(2):
+                for h in range(each):
                     nc.vector.tensor_scalar(
                         out=f[:, a, h, :],
                         in0=u[:, a, h, :],
@@ -170,40 +173,46 @@ def tile_rebasedlinearattention_pa_k_kernel(
                     )
             return f
 
-        def store(out_rows, c, f):
-            nc.sync.dma_start(
-                out=out_rows[:, c * N_TILE : (c + 1) * N_TILE], in_=f[:].rearrange("p a h d -> p (a h d)")
-            )
+        def store(out_rows, first, width, f):
+            nc.sync.dma_start(out=out_rows[:, first : first + width], in_=f[:].rearrange("p a h d -> p (a h d)"))
 
         q_words = Wq_words.rearrange("g p n t -> g p (n t)").bitcast(I32)
         k_words = Wk_words.rearrange("g p n t -> g p (n t)").bitcast(I32)
         q_out = out_0[0].rearrange("t h d -> t (h d)")
         k_out = out_1[0].rearrange("t h d -> t (h d)")
 
-        def whole_group(acc, g, words, planes):
+        def whole_group(accs, units, g, words, planes):
             w = wide.tile([P, N_OUT], U32, align_bytes=64)
             nc.sync.dma_start(out=w[:].bitcast(I32), in_=words[g])
-            for c in range(CHUNKS):
-                multiply(acc[c], g, w[:, c * N_TILE : (c + 1) * N_TILE], planes, c)
+            for acc, (first, width) in zip(accs, units):
+                multiply(acc, g, w[:, first : first + width], planes, first, width)
 
+        q_units = [(c * N_TILE, N_TILE) for c in range(CHUNKS)]
         acc_q = [psum_acc.tile([P, N_TILE], F32, name="acc_q%d" % c) for c in range(CHUNKS)]
         for g in range(GROUPS):
-            whole_group(acc_q, g, q_words, planes_q)
-        q_feat = [feature_map(acc_q[c], D**-0.5, shift_q) for c in range(CHUNKS)]
+            whole_group(acc_q, q_units, g, q_words, planes_q)
+        q_feat = [feature_map(acc_q[c], 4, D**-0.5, shift_q) for c in range(CHUNKS)]
 
-        acc_k = [psum_acc.tile([P, N_TILE], F32, name="acc_k%d" % c) for c in range(CHUNKS)]
+        acc_k = [psum_acc.tile([P, K_UNITS[i][1]], F32, name="acc_k%d" % i) for i in range(3)]
+        acc_last = psum_x.tile([P, K_UNITS[3][1]], F32, tag="bank")
+        acc_k.append(acc_last)
         for g in range(GROUPS - TAIL_GROUPS):
-            whole_group(acc_k, g, k_words, planes_k)
+            whole_group(acc_k, K_UNITS, g, k_words, planes_k)
         tail = {}
-        for c in range(CHUNKS):
-            for g in range(GROUPS - TAIL_GROUPS, GROUPS):
-                tail[(c, g)] = narrow.tile([P, N_TILE], U32, name="tail_%d_%d" % (c, g), align_bytes=64)
+        for i, (first, width) in enumerate(K_UNITS):
+            g = GROUPS - TAIL_GROUPS
+            for count in TAIL_LOADS[i]:
+                w = narrow.tile([P, count, width], U32, name="tail_%d_%d" % (i, g), align_bytes=64)
                 nc.sync.dma_start(
-                    out=tail[(c, g)][:].bitcast(I32), in_=k_words[g, :, c * N_TILE : (c + 1) * N_TILE]
+                    out=w[:].bitcast(I32),
+                    in_=k_words[g : g + count, :, first : first + width].rearrange("g p n -> p g n"),
                 )
+                for j in range(count):
+                    tail[(i, g + j)] = w[:, j, :]
+                g += count
         for c in range(CHUNKS):
-            store(q_out, c, q_feat[c])
-        for c in range(CHUNKS):
+            store(q_out, c * N_TILE, N_TILE, q_feat[c])
+        for i, (first, width) in enumerate(K_UNITS):
             for g in range(GROUPS - TAIL_GROUPS, GROUPS):
-                multiply(acc_k[c], g, tail[(c, g)][:], planes_k, c)
-            store(k_out, c, feature_map(acc_k[c], 1.0, shift_k))
+                multiply(acc_k[i], g, tail[(i, g)], planes_k, first, width)
+            store(k_out, first, width, feature_map(acc_k[i], width // D, 1.0, shift_k))

@@ -24,12 +24,12 @@ LN_EPS = 1e-5
 
 PLANES_PER_SLOT = 4
 SLOTS = GROUPS // PLANES_PER_SLOT
-X_PIECES = 4
+X_PIECES = 2
 GROUPS_PER_PIECE = GROUPS // X_PIECES
 GROUPS_PER_BANK = 2
-TAIL_GROUPS = 8
+TAIL_GROUPS = 6
 K_UNITS = [(0, 512), (512, 512), (1024, 256), (1280, 256)]
-TAIL_LOADS = [[1] * 8, [1] * 8, [2, 2, 2, 2], [2, 2, 2, 1, 1]]
+TAIL_LOADS = [[1] * 6, [1] * 6, [2, 2, 2], [2, 2, 1, 1]]
 
 FLOPS = 2 * P * HID * 2 * N_OUT
 
@@ -137,7 +137,7 @@ def tile_rebasedlinearattention_pa_k_kernel(
                 stop=(g == GROUPS - 1),
             )
 
-        def feature_map(acc, heads, factor, shift):
+        def feature_map(acc, heads, factor, shift, last=False):
             each = heads // 2
             v = acc[:].rearrange("p (a h d) -> p a h d", a=2, d=D)
             u = work.tile([P, 2, each, D], F32, tag="u%d" % each)
@@ -147,30 +147,54 @@ def tile_rebasedlinearattention_pa_k_kernel(
                 nc.vector.tensor_tensor(out=u[:, a], in0=u[:, a], in1=gb_rep(1, each), op=ALU.add)
             stats = small.tile([P, 2, each, 6], F32, tag="stats%d" % each)
             mean_var = small.tile([P, 2, each, 2], F32, tag="mean_var%d" % each)
+            minus_mean = small.tile([P, 2, each], F32, tag="minus_mean%d" % each)
             gain = small.tile([P, 2, each], F32, tag="gain%d" % each)
-            for a in range(2):
-                for h in range(each):
+            offset = small.tile([P, 2, each], F32, tag="offset%d" % each)
+            f = results.tile([P, 2, each, D], F32, tag="f%d" % each)
+            step = 3 - each
+            for first in range(0, 2, step):
+                halves = slice(first, first + step)
+                pair = [(a, h) for a in range(first, first + step) for h in range(each)]
+                for a, h in pair:
                     nc.vector.bn_stats(out=stats[:, a, h, :], in_=u[:, a, h, :])
-                for h in range(each):
+                for a, h in pair:
                     nc.vector.bn_aggr(out=mean_var[:, a, h, :], in_=stats[:, a, h, :])
                 nc.scalar.activation(
-                    out=gain[:, a, :],
-                    in_=mean_var[:, a, :, 1],
+                    out=gain[:, halves, :],
+                    in_=mean_var[:, halves, :, 1],
                     func=ACT.Abs_reciprocal_sqrt,
                     bias=shift[:, 0:1],
                     scale=1.0 / factor**2,
                 )
-            f = results.tile([P, 2, each, D], F32, tag="f%d" % each)
-            for a in range(2):
-                for h in range(each):
-                    nc.vector.tensor_scalar(
-                        out=f[:, a, h, :],
-                        in0=u[:, a, h, :],
-                        scalar1=mean_var[:, a, h, 0:1],
-                        scalar2=gain[:, a, h : h + 1],
-                        op0=ALU.subtract,
-                        op1=ALU.mult,
+                if last:
+                    for a, h in pair:
+                        nc.vector.tensor_scalar(
+                            out=f[:, a, h, :],
+                            in0=u[:, a, h, :],
+                            scalar1=mean_var[:, a, h, 0:1],
+                            scalar2=gain[:, a, h : h + 1],
+                            op0=ALU.subtract,
+                            op1=ALU.mult,
+                        )
+                else:
+                    nc.vector.tensor_scalar_mul(
+                        out=minus_mean[:, halves, :], in0=mean_var[:, halves, :, 0], scalar1=-1.0
                     )
+                    for a, h in pair:
+                        nc.scalar.activation(
+                            out=offset[:, a, h : h + 1],
+                            in_=minus_mean[:, a, h : h + 1],
+                            func=ACT.Copy,
+                            scale=gain[:, a, h : h + 1],
+                        )
+                    for a, h in pair:
+                        nc.scalar.activation(
+                            out=f[:, a, h, :],
+                            in_=u[:, a, h, :],
+                            func=ACT.Identity,
+                            bias=offset[:, a, h : h + 1],
+                            scale=gain[:, a, h : h + 1],
+                        )
             return f
 
         def store(out_rows, first, width, f):
@@ -215,4 +239,4 @@ def tile_rebasedlinearattention_pa_k_kernel(
         for i, (first, width) in enumerate(K_UNITS):
             for g in range(GROUPS - TAIL_GROUPS, GROUPS):
                 multiply(acc_k[i], g, tail[(i, g)], planes_k, first, width)
-            store(k_out, first, width, feature_map(acc_k[i], width // D, 1.0, shift_k))
+            store(k_out, first, width, feature_map(acc_k[i], width // D, 1.0, shift_k, last=i == len(K_UNITS) - 1))

@@ -21,6 +21,7 @@ N_OUT = 12 * D
 N_TILE = 512
 CHUNKS = N_OUT // N_TILE
 LN_EPS = 1e-5
+DMA_ALIGN = 256
 
 PLANES_PER_SLOT = 4
 SLOTS = GROUPS // PLANES_PER_SLOT
@@ -65,7 +66,7 @@ def tile_rebasedlinearattention_pa_k_kernel(
         piece_cols = HID // X_PIECES
         x_pieces = []
         for i in range(X_PIECES):
-            x_piece = xin.tile([P, piece_cols], BF16)
+            x_piece = xin.tile([P, piece_cols], BF16, align_bytes=DMA_ALIGN)
             nc.sync.dma_start(out=x_piece[:], in_=x_rows[:, i * piece_cols : (i + 1) * piece_cols])
             x_pieces.append(x_piece)
 
@@ -206,7 +207,7 @@ def tile_rebasedlinearattention_pa_k_kernel(
         k_out = out_1[0].rearrange("t h d -> t (h d)")
 
         def whole_group(accs, units, g, words, planes):
-            w = wide.tile([P, N_OUT], U32, align_bytes=64)
+            w = wide.tile([P, N_OUT], U32, align_bytes=DMA_ALIGN)
             nc.sync.dma_start(out=w[:].bitcast(I32), in_=words[g])
             for acc, (first, width) in zip(accs, units):
                 multiply(acc, g, w[:, first : first + width], planes, first, width)
@@ -226,7 +227,7 @@ def tile_rebasedlinearattention_pa_k_kernel(
         for i, (first, width) in enumerate(K_UNITS):
             g = GROUPS - TAIL_GROUPS
             for count in TAIL_LOADS[i]:
-                w = narrow.tile([P, count, width], U32, name="tail_%d_%d" % (i, g), align_bytes=64)
+                w = narrow.tile([P, count, width], U32, name="tail_%d_%d" % (i, g), align_bytes=DMA_ALIGN)
                 nc.sync.dma_start(
                     out=w[:].bitcast(I32),
                     in_=k_words[g : g + count, :, first : first + width].rearrange("g p n -> p g n"),

from contextlib import ExitStack

import concourse.mybir as mybir
from concourse.masks import make_identity

F32 = mybir.dt.float32
BF16 = mybir.dt.bfloat16
I32 = mybir.dt.int32
U32 = mybir.dt.uint32
U8 = mybir.dt.uint8
FP8X4 = mybir.dt.float8_e4m3fn_x4
ALU = mybir.AluOpType
ACT = mybir.ActivationFunctionType

P = 128
HID = 8192
K_PASS = 4 * P
GROUPS = HID // K_PASS
D = 128
N_OUT = 12 * D
N_TILE = 512
CHUNKS = N_OUT // N_TILE
LN_EPS = 1e-5
DMA_ALIGN = 256

PLANES_PER_SLOT = 4
SLOTS = GROUPS // PLANES_PER_SLOT
X_PIECES = 2
GROUPS_PER_PIECE = GROUPS // X_PIECES
GROUPS_PER_BANK = 2
TAIL_GROUPS = 6
K_UNITS = [(0, 512), (512, 512), (1024, 256), (1280, 256)]
TAIL_LOADS = [[1] * 6, [1] * 6, [2, 2, 2], [2, 2, 1, 1]]

FLOPS = 2 * P * HID * 2 * N_OUT


def tile_rebasedlinearattention_pa_k_kernel(
    tc, hidden_states, Wq_words, Wq_scales, Wk_words, Wk_scales, gamma, beta, out_0, out_1
):
    nc = tc.nc
    with ExitStack() as ctx:
        const = ctx.enter_context(tc.tile_pool(name="const", bufs=1))
        xin = ctx.enter_context(tc.tile_pool(name="xin", bufs=X_PIECES))
        stage = ctx.enter_context(tc.tile_pool(name="stage", bufs=3))
        wide = ctx.enter_context(tc.tile_pool(name="wide", bufs=12))
        narrow = ctx.enter_context(tc.tile_pool(name="narrow", bufs=1))
        work = ctx.enter_context(tc.tile_pool(name="work", bufs=3))
        results = ctx.enter_context(tc.tile_pool(name="results", bufs=2 * CHUNKS))
        small = ctx.enter_context(tc.tile_pool(name="small", bufs=3))
        psum_x = ctx.enter_context(tc.psum_pool(name="psum_x", bufs=2))
        psum_acc = ctx.enter_context(tc.psum_pool(name="psum_acc", bufs=1))
        ctx.enter_context(tc.manual_schedule())

        shift_q = const.tile([P, 1], F32)
        nc.vector.memset(shift_q[:], LN_EPS * D)
        shift_k = const.tile([P, 1], F32)
        nc.vector.memset(shift_k[:], LN_EPS)
        warm = const.tile([P, 1], F32)
        nc.scalar.activation(out=warm[:], in_=shift_k[:], func=ACT.Abs_reciprocal_sqrt)

        ident = const.tile([P, P], F32)
        make_identity(nc, ident[:])

        x_rows = hidden_states[0]
        piece_cols = HID // X_PIECES
        x_pieces = []
        for i in range(X_PIECES):
            x_piece = xin.tile([P, piece_cols], BF16, align_bytes=DMA_ALIGN)
            nc.sync.dma_start(out=x_piece[:], in_=x_rows[:, i * piece_cols : (i + 1) * piece_cols])
            x_pieces.append(x_piece)

        def load_scale_planes(planes, scales):
            nc.vector.memset(planes[:].bitcast(I32), 0)
            for j in range(SLOTS):
                for quadrant in range(4):
                    nc.gpsimd.dma_start(
                        out=planes[32 * quadrant : 32 * quadrant + 16, j, :].bitcast(F32),
                        in_=scales[
                            PLANES_PER_SLOT * j : PLANES_PER_SLOT * (j + 1),
                            4 * quadrant : 4 * quadrant + 4,
                            :,
                        ].bitcast(F32),
                    )

        planes_q = const.tile([P, SLOTS, N_OUT], U8, align_bytes=64)
        planes_k = const.tile([P, SLOTS, N_OUT], U8, align_bytes=64)
        load_scale_planes(planes_q, Wq_scales)
        load_scale_planes(planes_k, Wk_scales)

        gb_rows = const.tile([P, 2 * D], BF16)
        nc.vector.memset(gb_rows[:], 0.0)
        nc.scalar.dma_start(out=gb_rows[0:1, 0:D], in_=gamma.unsqueeze(0))
        nc.scalar.dma_start(out=gb_rows[0:1, D : 2 * D], in_=beta.unsqueeze(0))
        ones = const.tile([P, P], BF16)
        nc.vector.memset(ones[:], 1.0)

        x_codes = const.tile([P, GROUPS * P], U32, align_bytes=64)
        x_planes = const.tile([P, GROUPS * P], U8, align_bytes=64)
        for b in range(GROUPS // GROUPS_PER_BANK):
            xt = psum_x.tile([P, GROUPS_PER_BANK, 2, P], F32, tag="bank")
            for i in range(GROUPS_PER_BANK):
                g = GROUPS_PER_BANK * b + i
                pairs = x_pieces[g // GROUPS_PER_PIECE][:].bitcast(F32)
                first = (g % GROUPS_PER_PIECE) * (K_PASS // 2)
                for u in range(2):
                    nc.tensor.transpose(
                        xt[:, i, u, :], pairs[:, first + u : first + K_PASS // 2 : 2], ident[:]
                    )
            grouped = stage.tile([P, GROUPS_PER_BANK * K_PASS], BF16, align_bytes=64)
            nc.scalar.copy(
                out=grouped[:].bitcast(F32).rearrange("p (g t u) -> p g t u", g=GROUPS_PER_BANK, u=2),
                in_=xt[:].rearrange("p g u t -> p g t u"),
            )
            cols = slice(GROUPS_PER_BANK * b * P, GROUPS_PER_BANK * (b + 1) * P)
            nc.vector.quantize_mx(
                out=x_codes[:, cols].bitcast(FP8X4), scales=x_planes[:, cols], in_=grouped[:]
            )

        gb_bank = psum_x.tile([P, 2 * D], F32, tag="bank")
        nc.tensor.matmul(out=gb_bank[:], lhsT=ones[:], rhs=gb_rows[:], start=True, stop=True)
        gb = const.tile([P, 2, D], F32)
        nc.vector.tensor_copy(out=gb[:].rearrange("p a d -> p (a d)"), in_=gb_bank[:])

        def gb_rep(which, heads):
            return gb[:, which, :].unsqueeze(1).to_broadcast([P, heads, D])

        def multiply(acc, g, w_words, planes, first, width):
            nc.tensor.matmul_mx(
                out=acc[:],
                lhsT=x_codes[:, g * P : (g + 1) * P].bitcast(FP8X4),
                lhsT_scale=x_planes[:, g * P : (g + 1) * P],
                rhs=w_words.bitcast(FP8X4),
                rhs_scale=planes[
                    4 * (g % PLANES_PER_SLOT) : P, g // PLANES_PER_SLOT, first : first + width
                ],
                start=(g == 0),
                stop=(g == GROUPS - 1),
            )

        def feature_map(acc, heads, factor, shift, last=False):
            each = heads // 2
            v = acc[:].rearrange("p (a h d) -> p a h d", a=2, d=D)
            u = work.tile([P, 2, each, D], F32, tag="u%d" % each)
            for a in range(2):
                nc.vector.tensor_tensor(out=u[:, a], in0=v[:, a], in1=gb_rep(0, each), op=ALU.mult)
            for a in range(2):
                nc.vector.tensor_tensor(out=u[:, a], in0=u[:, a], in1=gb_rep(1, each), op=ALU.add)
            stats = small.tile([P, 2, each, 6], F32, tag="stats%d" % each)
            mean_var = small.tile([P, 2, each, 2], F32, tag="mean_var%d" % each)
            minus_mean = small.tile([P, 2, each], F32, tag="minus_mean%d" % each)
            gain = small.tile([P, 2, each], F32, tag="gain%d" % each)
            offset = small.tile([P, 2, each], F32, tag="offset%d" % each)
            f = results.tile([P, 2, each, D], F32, tag="f%d" % each)
            step = 3 - each
            for first in range(0, 2, step):
                halves = slice(first, first + step)
                pair = [(a, h) for a in range(first, first + step) for h in range(each)]
                for a, h in pair:
                    nc.vector.bn_stats(out=stats[:, a, h, :], in_=u[:, a, h, :])
                for a, h in pair:
                    nc.vector.bn_aggr(out=mean_var[:, a, h, :], in_=stats[:, a, h, :])
                nc.scalar.activation(
                    out=gain[:, halves, :],
                    in_=mean_var[:, halves, :, 1],
                    func=ACT.Abs_reciprocal_sqrt,
                    bias=shift[:, 0:1],
                    scale=1.0 / factor**2,
                )
                if last:
                    for a, h in pair:
                        nc.vector.tensor_scalar(
                            out=f[:, a, h, :],
                            in0=u[:, a, h, :],
                            scalar1=mean_var[:, a, h, 0:1],
                            scalar2=gain[:, a, h : h + 1],
                            op0=ALU.subtract,
                            op1=ALU.mult,
                        )
                else:
                    nc.vector.tensor_scalar_mul(
                        out=minus_mean[:, halves, :], in0=mean_var[:, halves, :, 0], scalar1=-1.0
                    )
                    for a, h in pair:
                        nc.scalar.activation(
                            out=offset[:, a, h : h + 1],
                            in_=minus_mean[:, a, h : h + 1],
                            func=ACT.Copy,
                            scale=gain[:, a, h : h + 1],
                        )
                    for a, h in pair:
                        nc.scalar.activation(
                            out=f[:, a, h, :],
                            in_=u[:, a, h, :],
                            func=ACT.Identity,
                            bias=offset[:, a, h : h + 1],
                            scale=gain[:, a, h : h + 1],
                        )
            return f

        def store(out_rows, first, width, f):
            nc.sync.dma_start(out=out_rows[:, first : first + width], in_=f[:].rearrange("p a h d -> p (a h d)"))

        q_words = Wq_words.rearrange("g p n t -> g p (n t)").bitcast(I32)
        k_words = Wk_words.rearrange("g p n t -> g p (n t)").bitcast(I32)
        q_out = out_0[0].rearrange("t h d -> t (h d)")
        k_out = out_1[0].rearrange("t h d -> t (h d)")

        def whole_group(accs, units, g, words, planes):
            w = wide.tile([P, N_OUT], U32, align_bytes=DMA_ALIGN)
            nc.sync.dma_start(out=w[:].bitcast(I32), in_=words[g])
            for acc, (first, width) in zip(accs, units):
                multiply(acc, g, w[:, first : first + width], planes, first, width)

        q_units = [(c * N_TILE, N_TILE) for c in range(CHUNKS)]
        acc_q = [psum_acc.tile([P, N_TILE], F32, name="acc_q%d" % c) for c in range(CHUNKS)]
        for g in range(GROUPS):
            whole_group(acc_q, q_units, g, q_words, planes_q)
        q_feat = [feature_map(acc_q[c], 4, D**-0.5, shift_q) for c in range(CHUNKS)]

        acc_k = [psum_acc.tile([P, K_UNITS[i][1]], F32, name="acc_k%d" % i) for i in range(3)]
        acc_last = psum_x.tile([P, K_UNITS[3][1]], F32, tag="bank")
        acc_k.append(acc_last)
        for g in range(GROUPS - TAIL_GROUPS):
            whole_group(acc_k, K_UNITS, g, k_words, planes_k)
        tail = {}
        for i, (first, width) in enumerate(K_UNITS):
            g = GROUPS - TAIL_GROUPS
            for count in TAIL_LOADS[i]:
                w = narrow.tile([P, count, width], U32, name="tail_%d_%d" % (i, g), align_bytes=DMA_ALIGN)
                nc.sync.dma_start(
                    out=w[:].bitcast(I32),
                    in_=k_words[g : g + count, :, first : first + width].rearrange("g p n -> p g n"),
                )
                for j in range(count):
                    tail[(i, g + j)] = w[:, j, :]
                g += count
        for c in range(CHUNKS):
            store(q_out, c * N_TILE, N_TILE, q_feat[c])
        for i, (first, width) in enumerate(K_UNITS):
            for g in range(GROUPS - TAIL_GROUPS, GROUPS):
                multiply(acc_k[i], g, tail[(i, g)], planes_k, first, width)
            store(k_out, first, width, feature_map(acc_k[i], width // D, 1.0, shift_k, last=i == len(K_UNITS) - 1))
